import numpy as np
import ml_dtypes


def mxq(x, axis, fmt="e4m3"):
    dtype, down = {"e4m3": (ml_dtypes.float8_e4m3fn, 7), "e5m2": (ml_dtypes.float8_e5m2, 14)}[fmt]
    v = np.moveaxis(np.asarray(x, np.float32).astype(ml_dtypes.bfloat16).astype(np.float64), axis, -1)
    blocks = v.reshape(v.shape[:-1] + (-1, 32))
    amax = np.abs(blocks).max(-1, keepdims=True)
    byte = np.maximum(np.where(amax > 0, np.frexp(amax)[1] - 1 + 127, 0) - down, 1)
    scale = np.exp2(byte - 127.0)
    codes = (blocks / scale).astype(np.float32).astype(dtype).astype(np.float64)
    return np.moveaxis((codes * scale).reshape(v.shape), -1, axis)


WIDE = False


def mx_kscale(k):
    if not WIDE:
        return np.ones(k)
    levels = np.array([30, -30])
    if k % 512:
        return np.exp2(np.random.permutation(np.resize(levels, k // 32))).repeat(32)
    a = np.empty((k // 512, 16))
    for p in range(k // 512):
        a[p, :8] = np.random.permutation(np.resize(levels, 8))
        for g in range(8):
            far = levels[np.abs(levels - a[p, g]) >= 10]
            a[p, g + 8] = far[np.random.randint(len(far))]
    return np.exp2(a.ravel()).repeat(32)


BF16 = ml_dtypes.bfloat16


def bf(x):
    return np.asarray(x, np.float32).astype(BF16)


def f64(x):
    return np.asarray(x).astype(np.float64)


B, F, H, W, NH, DH, P, SINK, LOCAL = 1, 4, 16, 32, 8, 128, 1024, 1, 2
D = NH * DH
L = F * H * W
C = DH // 2
C1 = C // 3
C0 = C - 2 * C1
THETA = 1.0e4
EPS = 1.0e-6


def rope_params(n):
    inv = 1.0 / THETA ** (np.arange(0, 2 * n, 2) / (2 * n))
    ang = np.outer(np.arange(P), inv)
    return np.stack([np.cos(ang), np.sin(ang)], -1)


def setup_inputs():
    s = mx_kscale(D)
    freqs = np.concatenate([rope_params(C0), rope_params(C1), rope_params(C1)], axis=1)
    return {
        "x": bf(np.random.standard_normal((B, L, D)) * s),
        "wq": bf(np.random.standard_normal((D, D)) / np.sqrt(D) / s),
        "bq": bf(np.random.standard_normal(D) * 0.3),
        "wk": bf(np.random.standard_normal((D, D)) / np.sqrt(D) / s),
        "bk": bf(np.random.standard_normal(D) * 0.3),
        "gq": bf(1.5 * (1.0 + 0.1 * np.random.standard_normal(D))),
        "gk": bf(1.5 * (1.0 + 0.1 * np.random.standard_normal(D))),
        "freqs": bf(freqs),
    }


def rmsnorm(t, g):
    return t * (1.0 / np.sqrt(np.mean(t * t, -1, keepdims=True) + EPS)) * g


def rope_table(fr):
    ft = np.broadcast_to(fr[:F, :C0].reshape(F, 1, 1, C0, 2), (F, H, W, C0, 2))
    fh = np.broadcast_to(fr[:H, C0:C0 + C1].reshape(1, H, 1, C1, 2), (F, H, W, C1, 2))
    fw = np.broadcast_to(fr[:W, C0 + C1:].reshape(1, 1, W, C1, 2), (F, H, W, C1, 2))
    return np.concatenate([ft, fh, fw], -2).reshape(L, C, 2)


def apply_rope(t, fr):
    tr = t.reshape(B, L, NH, C, 2)
    a, b = tr[..., 0], tr[..., 1]
    cos = fr[None, :, None, :, 0]
    sin = fr[None, :, None, :, 1]
    return np.stack([a * cos - b * sin, a * sin + b * cos], -1).reshape(B, L, NH, DH)


def reference(x, wq, bq, wk, bk, gq, gk, freqs):
    xq = mxq(f64(x), 2, "e5m2")
    q = rmsnorm((xq @ mxq(f64(wq), 1, "e5m2").T) + f64(bq), f64(gq))
    k = rmsnorm((xq @ mxq(f64(wk), 1, "e5m2").T) + f64(bk), f64(gk))
    fr = rope_table(f64(freqs))
    return apply_rope(q, fr), apply_rope(k, fr)

@@ -1,0 +1,282 @@
+from contextlib import ExitStack
+
+import concourse.mybir as mybir
+from concourse.masks import make_identity
+
+F32 = mybir.dt.float32
+BF16 = mybir.dt.bfloat16
+U32 = mybir.dt.uint32
+U8 = mybir.dt.uint8
+E5X4 = mybir.dt.float8_e5m2_x4
+ALU = mybir.AluOpType
+ACT = mybir.ActivationFunctionType
+
+P = 128
+L = 2048
+D = 1024
+EPS = 1.0e-6
+FC = 44
+HC = 86
+FLOPS = 2 * L * D * 2 * D
+
+
+def tile_causalwanselfattention_pa_kernel(tc, x, wq, bq, wk, bk, gq, gk, freqs, out_0, out_1):
+    nc = tc.nc
+    xf = x.flatten_outer_dims()
+    outs = (out_0.rearrange("b l h d -> (b l) (h d)"), out_1.rearrange("b l h d -> (b l) (h d)"))
+    wsrc = (wq, wk)
+
+    with ExitStack() as ctx:
+        const = ctx.enter_context(tc.tile_pool(name="const", bufs=1))
+        rawp = ctx.enter_context(tc.tile_pool(name="rawp", bufs=12))
+        grpp = ctx.enter_context(tc.tile_pool(name="grpp", bufs=2))
+        keep = ctx.enter_context(tc.tile_pool(name="keep", bufs=1))
+        ttp = ctx.enter_context(tc.tile_pool(name="ttp", bufs=16))
+        work = ctx.enter_context(tc.tile_pool(name="work", bufs=2))
+        outp = ctx.enter_context(tc.tile_pool(name="outp", bufs=3))
+        small = ctx.enter_context(tc.tile_pool(name="small", bufs=4))
+        ps_mm = ctx.enter_context(tc.psum_pool(name="ps_mm", bufs=2))
+        ps_tp = ctx.enter_context(tc.psum_pool(name="ps_tp", bufs=4))
+        ps_in = ctx.enter_context(tc.psum_pool(name="ps_in", bufs=2))
+
+        one = const.tile([P, 1], F32, name="one")
+        nc.vector.memset(one[:], 1.0)
+        warm = const.tile([P, 1], F32, name="warm")
+        nc.scalar.activation(out=warm[:], in_=one[:], func=ACT.Sqrt)
+
+        misc = const.tile([P, P], BF16, name="misc")
+        nc.vector.memset(misc[:], 0.0)
+        for i, v in enumerate((bq, bk, gq, gk)):
+            nc.scalar.dma_start(out=misc[8 * i : 8 * i + 8, :], in_=v.rearrange("(r c) -> r c", c=P))
+        fr = const.tile([P, P], BF16, name="fr")
+        nc.scalar.dma_start(out=fr[:], in_=freqs[0:P].rearrange("p j t -> p (j t)"))
+
+        identb = const.tile([P, P], BF16, name="identb")
+        make_identity(nc, identb[:])
+        identf = const.tile([P, P], F32, name="identf")
+        make_identity(nc, identf[:])
+
+        raws = {}
+
+        def load(key, rows):
+            t = rawp.tile([P, D], BF16, name="raw", tag="raw")
+            nc.sync.dma_start(out=t[:], in_=rows)
+            raws[key] = t
+
+        def load_x(i):
+            load(("x", i), xf[P * i : P * (i + 1), :])
+
+        def load_w(ft):
+            load(("w", ft), wsrc[ft // 8][P * (ft % 8) : P * (ft % 8 + 1), :])
+
+        for i in range(4):
+            load_x(i)
+        for ft in range(8):
+            load_w(ft)
+
+        selw = const.tile([P, 4, 32], BF16, name="selw")
+        nc.vector.tensor_copy(out=selw[:], in_=identb[:, 0:32].unsqueeze(1).to_broadcast([P, 4, 32]))
+        selh = const.tile([P, 16, 32], BF16, name="selh")
+        nc.vector.tensor_copy(out=selh[:], in_=identb[:, 0:16].unsqueeze(2).to_broadcast([P, 16, 32]))
+
+        bt_ps = ps_in.tile([P, P], BF16, name="bt_ps", tag="in")
+        nc.tensor.transpose(bt_ps[:], misc[:], identb[:])
+        bcol = const.tile([P, 16], F32, name="bcol")
+        nc.vector.tensor_copy(out=bcol[:], in_=bt_ps[:, 0:16])
+
+        cs_ps = ps_in.tile([P, 4, P], F32, name="cs_ps", tag="in")
+        for r in range(4):
+            nc.tensor.matmul(cs_ps[:, r, 0:FC], lhsT=identb[:, r : r + 1].to_broadcast([P, P]), rhs=fr[:, 0:FC], start=True, stop=True)
+            nc.tensor.matmul(cs_ps[:, r, FC:HC], lhsT=selh[:, 4 * r : 4 * r + 4, :].rearrange("k a w -> k (a w)"), rhs=fr[:, FC:HC], start=True, stop=True)
+            nc.tensor.matmul(cs_ps[:, r, HC:P], lhsT=selw[:].rearrange("k a w -> k (a w)"), rhs=fr[:, HC:P], start=True, stop=True)
+        cc = const.tile([P, 4, P], F32, name="cc")
+        ss = const.tile([P, 4, P], F32, name="ss")
+        csv = cs_ps[:].rearrange("p r (j t) -> p (r j) t", t=2)
+        ssv = ss[:].rearrange("p r (j t) -> p (r j) t", t=2)
+        nc.vector.tensor_copy(out=cc[:].rearrange("p r (j t) -> p (r j) t", t=2), in_=csv[:, :, 0:1].to_broadcast([P, 256, 2]))
+        nc.vector.tensor_copy(out=ssv[:, :, 0:1], in_=csv[:, :, 1:2])
+        nc.vector.tensor_scalar_mul(out=ssv[:, :, 1:2], in0=csv[:, :, 1:2], scalar1=-1.0)
+        trig = (cc, ss)
+
+        g_ps = []
+        for b in range(4):
+            gp = ps_tp.tile([P, 4, P], F32, name="g_ps", tag="tp")
+            for hh in range(4):
+                i = 16 + 4 * b + hh
+                nc.tensor.matmul(gp[:, hh, :], lhsT=identb[:, i : i + 1].to_broadcast([P, P]), rhs=misc[:], start=True, stop=True)
+            g_ps.append(gp)
+        gb = const.tile([P, 16, P], F32, name="gb")
+        for b in (2, 3, 0, 1):
+            nc.scalar.copy(out=gb[:, 4 * b : 4 * b + 4, :], in_=g_ps[b][:])
+
+        tf = [const.tile([P, 2, 16, FC], F32, name="tf%d" % f) for f in range(4)]
+        thw = [const.tile([P, 2, 16, P - FC], F32, name="thw%d" % r) for r in range(4)]
+
+        def table_v(dst, v, lo, hi, b):
+            for which in range(2):
+                nc.vector.tensor_tensor(
+                    out=dst[:, which, 4 * b : 4 * b + 4, :],
+                    in0=g_ps[b][:, :, lo:hi],
+                    in1=trig[which][:, v, lo:hi].unsqueeze(1).to_broadcast([P, 4, hi - lo]),
+                    op=ALU.mult,
+                )
+
+        def table_g(dst, v, lo, hi, which, h0):
+            nc.gpsimd.tensor_tensor(
+                out=dst[:, which, h0 : h0 + 8, :],
+                in0=gb[:, h0 : h0 + 8, lo:hi],
+                in1=trig[which][:, v, lo:hi].unsqueeze(1).to_broadcast([P, 8, hi - lo]),
+                op=ALU.mult,
+            )
+
+        turn_count = {"n": 0}
+
+        def turn(key, dst_words):
+            words = raws[key][:].bitcast(F32)
+            ps = ps_in.tile([P, 2, 2, P], F32, name="in_ps", tag="in")
+            for g in range(2):
+                for u in range(2):
+                    nc.tensor.transpose(ps[:, g, u, :], words[:, 256 * g + u : 256 * (g + 1) : 2], identf[:])
+            src = ps[:].rearrange("p g u r -> p g r u")
+            if turn_count["n"] % 2 == 0:
+                nc.vector.tensor_copy(out=dst_words, in_=src)
+            else:
+                nc.scalar.copy(out=dst_words, in_=src)
+            turn_count["n"] += 1
+
+        grps = {}
+        xc = {}
+        xs = {}
+        wc = {}
+        ws = {}
+
+        def new_group(key):
+            grps[key] = grpp.tile([P, 4096], BF16, name="grp", tag="grp", align_bytes=64)
+
+        def turn_x(c, r):
+            gw = grps[("x", c)][:].bitcast(F32).rearrange("p (g t u) -> p g t u", g=2, u=2)
+            turn(("x", 4 * c + r), gw[:, :, P * r : P * (r + 1), :])
+
+        def turn_w(ft):
+            gw = grps[("w", ft // 4)][:].bitcast(F32).rearrange("p (a g m u) -> p a g m u", a=4, g=2, u=2)
+            turn(("w", ft), gw[:, ft % 4])
+
+        def quantize(key, codes, scales, nm):
+            codes[key[1]] = keep.tile([P, 1024], U32, name="c_%s%d" % (nm, key[1]), align_bytes=64)
+            scales[key[1]] = keep.tile([P, 1024], U8, name="s_%s%d" % (nm, key[1]), align_bytes=64)
+            nc.vector.quantize_mx(out=codes[key[1]][:].bitcast(E5X4), scales=scales[key[1]][:], in_=grps[key][:])
+
+        new_group(("x", 0))
+        for r in range(4):
+            turn_x(0, r)
+            load_w(8 + r)
+        quantize(("x", 0), xc, xs, "x")
+        for grp in range(2):
+            new_group(("w", grp))
+            for a in range(4):
+                turn_w(4 * grp + a)
+                if grp == 0:
+                    load_w(12 + a)
+                else:
+                    load_x(4 + a)
+            quantize(("w", grp), wc, ws, "w")
+
+        for b in range(2):
+            table_v(tf[0], 0, 0, FC, b)
+        for r in range(4):
+            for b in range(2):
+                table_v(thw[r], r, FC, P, b)
+        for which in range(2):
+            table_g(tf[0], 0, 0, FC, which, 8)
+        for r in range(4):
+            for which in range(2):
+                table_g(thw[r], r, FC, P, which, 8)
+
+        tts = {}
+
+        def mxe(s, h):
+            c = s // 2
+            ft = 8 * (s % 2) + h
+            col = (2 * (ft % 4)) * P
+            acc = ps_mm.tile([P, 512], F32, name="acc", tag="mm")
+            for g in range(2):
+                nc.tensor.matmul_mx(
+                    out=acc[:],
+                    lhsT=wc[ft // 4][:, col + P * g : col + P * (g + 1)].bitcast(E5X4),
+                    lhsT_scale=ws[ft // 4][:, col + P * g : col + P * (g + 1)],
+                    rhs=xc[c][:, 512 * g : 512 * (g + 1)].bitcast(E5X4),
+                    rhs_scale=xs[c][:, 512 * g : 512 * (g + 1)],
+                    start=(g == 0),
+                    stop=(g == 1),
+                )
+            tt = ttp.tile([P, 512], F32, name="tt", tag="tt")
+            nc.scalar.activation(out=tt[:], in_=acc[:], func=ACT.Identity, bias=bcol[:, ft : ft + 1], scale=1.0)
+            tts[(s, h)] = tt
+
+        def unit(s, r):
+            c = s // 2
+            qk = s % 2
+            tps = []
+            for b in range(2):
+                tp = ps_tp.tile([P, 512], F32, name="tp", tag="tp")
+                for hh in range(4):
+                    nc.tensor.transpose(tp[:, P * hh : P * (hh + 1)], tts[(s, 4 * b + hh)][:, P * r : P * (r + 1)], identf[:])
+                tps.append(tp)
+            ms = small.tile([P, 4], F32, name="ms", tag="ms")
+            for b in range(2):
+                junk = work.tile([P, 512], BF16, name="junk", tag="junk")
+                nc.scalar.activation(out=junk[:], in_=tps[b][:], func=ACT.Square, scale=1.0 / 32.0, accum_out=ms[:, b : b + 1])
+            nc.scalar.activation(out=ms[:, 2:3], in_=ms[:, 1:2], func=ACT.Identity, bias=EPS, scale=1.0)
+            nc.scalar.activation(out=ms[:, 3:4], in_=ms[:, 0:1], func=ACT.Sqrt, bias=ms[:, 2:3], scale=1.0)
+            rstd = small.tile([P, 1], F32, name="rstd", tag="rstd")
+            nc.vector.reciprocal(out=rstd[:], in_=ms[:, 3:4])
+
+            m1 = work.tile([P, D], F32, name="m1", tag="m1")
+            m2 = work.tile([P, D], F32, name="m2", tag="m2")
+            ms12 = (m1, m2)
+            for b in range(2):
+                tpv = tps[b][:].rearrange("p (h d) -> p h d", h=4)
+                h0 = 8 * qk + 4 * b
+                for which in range(2):
+                    mv = ms12[which][:].rearrange("p (h d) -> p h d", h=8)[:, 4 * b : 4 * b + 4, :]
+                    nc.vector.scalar_tensor_tensor(
+                        out=mv[:, :, 0:FC], in0=tpv[:, :, 0:FC], scalar=rstd[:, 0:1], in1=tf[c][:, which, h0 : h0 + 4, :],
+                        op0=ALU.mult, op1=ALU.mult,
+                    )
+                    nc.vector.scalar_tensor_tensor(
+                        out=mv[:, :, FC:P], in0=tpv[:, :, FC:P], scalar=rstd[:, 0:1], in1=thw[r][:, which, h0 : h0 + 4, :],
+                        op0=ALU.mult, op1=ALU.mult,
+                    )
+            o = outp.tile([P, D], F32, name="o", tag="o")
+            nc.gpsimd.tensor_tensor(
+                out=o[:].rearrange("p (c t) -> p c t", t=2),
+                in0=m1[:].rearrange("p (c t) -> p c t", t=2),
+                in1=m2[:].rearrange("p (c t) -> p c t", t=2)[:, :, ::-1],
+                op=ALU.add,
+            )
+            i = 4 * c + r
+            nc.sync.dma_start(out=outs[qk][P * i : P * (i + 1), :], in_=o[:])
+
+        for s in range(9):
+            for r in range(4):
+                if s < 8:
+                    mxe(s, 2 * r)
+                    mxe(s, 2 * r + 1)
+                if s == 0:
+                    if r % 2 == 0:
+                        new_group(("w", 2 + r // 2))
+                    for ft in (8 + 2 * r, 9 + 2 * r):
+                        turn_w(ft)
+                        load_x(ft)
+                    if r % 2 == 1:
+                        quantize(("w", 2 + r // 2), wc, ws, "w")
+                if s in (1, 3, 5):
+                    c = (s + 1) // 2
+                    if r == 0:
+                        new_group(("x", c))
+                    turn_x(c, r)
+                    if r == 3:
+                        quantize(("x", c), xc, xs, "x")
+                    table_g(tf[c], c, 0, FC, r % 2, 8 * (r // 2))
+                if s >= 1:
+                    unit(s - 1, r)

@@ -18,6 +18,8 @@ EPS = 1.0e-6
 FC = 44
 HC = 86
 FLOPS = 2 * L * D * 2 * D
+LAG_FRONT = 4
+LAG_BACK = 5
 
 
 def tile_causalwanselfattention_pa_kernel(tc, x, wq, bq, wk, bk, gq, gk, freqs, out_0, out_1):
@@ -32,29 +34,30 @@ def tile_causalwanselfattention_pa_kernel(tc, x, wq, bq, wk, bk, gq, gk, freqs, 
         grpp = ctx.enter_context(tc.tile_pool(name="grpp", bufs=2))
         keep = ctx.enter_context(tc.tile_pool(name="keep", bufs=1))
         ttp = ctx.enter_context(tc.tile_pool(name="ttp", bufs=16))
-        work = ctx.enter_context(tc.tile_pool(name="work", bufs=2))
+        work = ctx.enter_context(tc.tile_pool(name="work", bufs=3))
         outp = ctx.enter_context(tc.tile_pool(name="outp", bufs=3))
         small = ctx.enter_context(tc.tile_pool(name="small", bufs=4))
-        ps_mm = ctx.enter_context(tc.psum_pool(name="ps_mm", bufs=2))
-        ps_tp = ctx.enter_context(tc.psum_pool(name="ps_tp", bufs=4))
-        ps_in = ctx.enter_context(tc.psum_pool(name="ps_in", bufs=2))
+        psum = ctx.enter_context(tc.psum_pool(name="psum", bufs=1))
 
-        one = const.tile([P, 1], F32, name="one")
-        nc.vector.memset(one[:], 1.0)
-        warm = const.tile([P, 1], F32, name="warm")
-        nc.scalar.activation(out=warm[:], in_=one[:], func=ACT.Sqrt)
+        def bank(n, shape, dtype):
+            return psum.tile(shape, dtype, name="bank%d" % n, tag="bank%d" % n)
 
         misc = const.tile([P, P], BF16, name="misc")
-        nc.vector.memset(misc[:], 0.0)
         for i, v in enumerate((bq, bk, gq, gk)):
             nc.scalar.dma_start(out=misc[8 * i : 8 * i + 8, :], in_=v.rearrange("(r c) -> r c", c=P))
         fr = const.tile([P, P], BF16, name="fr")
         nc.scalar.dma_start(out=fr[:], in_=freqs[0:P].rearrange("p j t -> p (j t)"))
+        nc.vector.memset(misc[32:64, :], 0.0)
+        nc.vector.memset(misc[64:128, :], 0.0)
+        one = const.tile([P, 1], F32, name="one")
+        nc.vector.memset(one[:], 1.0)
+        warm = const.tile([P, 1], F32, name="warm")
+        nc.scalar.activation(out=warm[:], in_=one[:], func=ACT.Abs_reciprocal_sqrt)
 
-        identb = const.tile([P, P], BF16, name="identb")
-        make_identity(nc, identb[:])
         identf = const.tile([P, P], F32, name="identf")
         make_identity(nc, identf[:])
+        identb = const.tile([P, P], BF16, name="identb")
+        make_identity(nc, identb[:])
 
         raws = {}
 
@@ -74,17 +77,57 @@ def tile_causalwanselfattention_pa_kernel(tc, x, wq, bq, wk, bk, gq, gk, freqs, 
         for ft in range(8):
             load_w(ft)
 
+        def turn(key, dst_words, n, on_vector):
+            words = raws[key][:].bitcast(F32)
+            ps = bank(n, [P, 2, 2, P], F32)
+            for g in range(2):
+                for u in range(2):
+                    nc.tensor.transpose(ps[:, g, u, :], words[:, 256 * g + u : 256 * (g + 1) : 2], identf[:])
+            src = ps[:].rearrange("p g u r -> p g r u")
+            if on_vector:
+                nc.vector.tensor_copy(out=dst_words, in_=src)
+            else:
+                nc.scalar.copy(out=dst_words, in_=src)
+
+        grps = {}
+        xc = {}
+        xs = {}
+        wc = {}
+        ws = {}
+
+        def new_group(key):
+            grps[key] = grpp.tile([P, 4096], BF16, name="grp", tag="grp", align_bytes=64)
+
+        def turn_x(c, r, n, on_vector):
+            gw = grps[("x", c)][:].bitcast(F32).rearrange("p (g t u) -> p g t u", g=2, u=2)
+            turn(("x", 4 * c + r), gw[:, :, P * r : P * (r + 1), :], n, on_vector)
+
+        def turn_w(ft, n, on_vector):
+            gw = grps[("w", ft // 4)][:].bitcast(F32).rearrange("p (a g m u) -> p a g m u", a=4, g=2, u=2)
+            turn(("w", ft), gw[:, ft % 4], n, on_vector)
+
+        def quantize(key, codes, scales, nm):
+            codes[key[1]] = keep.tile([P, 1024], U32, name="c_%s%d" % (nm, key[1]), align_bytes=64)
+            scales[key[1]] = keep.tile([P, 1024], U8, name="s_%s%d" % (nm, key[1]), align_bytes=64)
+            nc.vector.quantize_mx(out=codes[key[1]][:].bitcast(E5X4), scales=scales[key[1]][:], in_=grps[key][:])
+
+        new_group(("x", 0))
+        for r in range(4):
+            turn_x(0, r, r, r % 2 == 0)
+            load_w(8 + r)
+        quantize(("x", 0), xc, xs, "x")
+
         selw = const.tile([P, 4, 32], BF16, name="selw")
         nc.vector.tensor_copy(out=selw[:], in_=identb[:, 0:32].unsqueeze(1).to_broadcast([P, 4, 32]))
         selh = const.tile([P, 16, 32], BF16, name="selh")
         nc.vector.tensor_copy(out=selh[:], in_=identb[:, 0:16].unsqueeze(2).to_broadcast([P, 16, 32]))
 
-        bt_ps = ps_in.tile([P, P], BF16, name="bt_ps", tag="in")
+        bt_ps = bank(4, [P, P], BF16)
         nc.tensor.transpose(bt_ps[:], misc[:], identb[:])
         bcol = const.tile([P, 16], F32, name="bcol")
         nc.vector.tensor_copy(out=bcol[:], in_=bt_ps[:, 0:16])
 
-        cs_ps = ps_in.tile([P, 4, P], F32, name="cs_ps", tag="in")
+        cs_ps = bank(5, [P, 4, P], F32)
         for r in range(4):
             nc.tensor.matmul(cs_ps[:, r, 0:FC], lhsT=identb[:, r : r + 1].to_broadcast([P, P]), rhs=fr[:, 0:FC], start=True, stop=True)
             nc.tensor.matmul(cs_ps[:, r, FC:HC], lhsT=selh[:, 4 * r : 4 * r + 4, :].rearrange("k a w -> k (a w)"), rhs=fr[:, FC:HC], start=True, stop=True)
@@ -98,14 +141,14 @@ def tile_causalwanselfattention_pa_kernel(tc, x, wq, bq, wk, bk, gq, gk, freqs, 
         nc.vector.tensor_scalar_mul(out=ssv[:, :, 1:2], in0=csv[:, :, 1:2], scalar1=-1.0)
         trig = (cc, ss)
 
-        g_ps = []
-        for b in range(4):
-            gp = ps_tp.tile([P, 4, P], F32, name="g_ps", tag="tp")
+        g_ps = {}
+        gb = const.tile([P, 16, P], F32, name="gb")
+        for b, n in ((0, 6), (1, 7), (2, 4), (3, 5)):
+            gp = bank(n, [P, 4, P], F32)
             for hh in range(4):
                 i = 16 + 4 * b + hh
                 nc.tensor.matmul(gp[:, hh, :], lhsT=identb[:, i : i + 1].to_broadcast([P, P]), rhs=misc[:], start=True, stop=True)
-            g_ps.append(gp)
-        gb = const.tile([P, 16, P], F32, name="gb")
+            g_ps[b] = gp
         for b in (2, 3, 0, 1):
             nc.scalar.copy(out=gb[:, 4 * b : 4 * b + 4, :], in_=g_ps[b][:])
 
@@ -129,52 +172,10 @@ def tile_causalwanselfattention_pa_kernel(tc, x, wq, bq, wk, bk, gq, gk, freqs, 
                 op=ALU.mult,
             )
 
-        turn_count = {"n": 0}
-
-        def turn(key, dst_words):
-            words = raws[key][:].bitcast(F32)
-            ps = ps_in.tile([P, 2, 2, P], F32, name="in_ps", tag="in")
-            for g in range(2):
-                for u in range(2):
-                    nc.tensor.transpose(ps[:, g, u, :], words[:, 256 * g + u : 256 * (g + 1) : 2], identf[:])
-            src = ps[:].rearrange("p g u r -> p g r u")
-            if turn_count["n"] % 2 == 0:
-                nc.vector.tensor_copy(out=dst_words, in_=src)
-            else:
-                nc.scalar.copy(out=dst_words, in_=src)
-            turn_count["n"] += 1
-
-        grps = {}
-        xc = {}
-        xs = {}
-        wc = {}
-        ws = {}
-
-        def new_group(key):
-            grps[key] = grpp.tile([P, 4096], BF16, name="grp", tag="grp", align_bytes=64)
-
-        def turn_x(c, r):
-            gw = grps[("x", c)][:].bitcast(F32).rearrange("p (g t u) -> p g t u", g=2, u=2)
-            turn(("x", 4 * c + r), gw[:, :, P * r : P * (r + 1), :])
-
-        def turn_w(ft):
-            gw = grps[("w", ft // 4)][:].bitcast(F32).rearrange("p (a g m u) -> p a g m u", a=4, g=2, u=2)
-            turn(("w", ft), gw[:, ft % 4])
-
-        def quantize(key, codes, scales, nm):
-            codes[key[1]] = keep.tile([P, 1024], U32, name="c_%s%d" % (nm, key[1]), align_bytes=64)
-            scales[key[1]] = keep.tile([P, 1024], U8, name="s_%s%d" % (nm, key[1]), align_bytes=64)
-            nc.vector.quantize_mx(out=codes[key[1]][:].bitcast(E5X4), scales=scales[key[1]][:], in_=grps[key][:])
-
-        new_group(("x", 0))
-        for r in range(4):
-            turn_x(0, r)
-            load_w(8 + r)
-        quantize(("x", 0), xc, xs, "x")
         for grp in range(2):
             new_group(("w", grp))
             for a in range(4):
-                turn_w(4 * grp + a)
+                turn_w(4 * grp + a, a, a % 2 == 0)
                 if grp == 0:
                     load_w(12 + a)
                 else:
@@ -193,12 +194,17 @@ def tile_causalwanselfattention_pa_kernel(tc, x, wq, bq, wk, bk, gq, gk, freqs, 
                 table_g(thw[r], r, FC, P, which, 8)
 
         tts = {}
+        mmb = {"n": 0}
+
+        def next_mm_bank():
+            mmb["n"] += 1
+            return mmb["n"] % 2
 
         def mxe(s, h):
             c = s // 2
             ft = 8 * (s % 2) + h
             col = (2 * (ft % 4)) * P
-            acc = ps_mm.tile([P, 512], F32, name="acc", tag="mm")
+            acc = bank(next_mm_bank(), [P, 512], F32)
             for g in range(2):
                 nc.tensor.matmul_mx(
                     out=acc[:],
@@ -213,12 +219,14 @@ def tile_causalwanselfattention_pa_kernel(tc, x, wq, bq, wk, bk, gq, gk, freqs, 
             nc.scalar.activation(out=tt[:], in_=acc[:], func=ACT.Identity, bias=bcol[:, ft : ft + 1], scale=1.0)
             tts[(s, h)] = tt
 
-        def unit(s, r):
-            c = s // 2
-            qk = s % 2
+        live = {}
+
+        def front(u):
+            s = u // 4
+            r = u % 4
             tps = []
             for b in range(2):
-                tp = ps_tp.tile([P, 512], F32, name="tp", tag="tp")
+                tp = bank(2 + 2 * (u % 3) + b, [P, 512], F32)
                 for hh in range(4):
                     nc.tensor.transpose(tp[:, P * hh : P * (hh + 1)], tts[(s, 4 * b + hh)][:, P * r : P * (r + 1)], identf[:])
                 tps.append(tp)
@@ -227,10 +235,16 @@ def tile_causalwanselfattention_pa_kernel(tc, x, wq, bq, wk, bk, gq, gk, freqs, 
                 junk = work.tile([P, 512], BF16, name="junk", tag="junk")
                 nc.scalar.activation(out=junk[:], in_=tps[b][:], func=ACT.Square, scale=1.0 / 32.0, accum_out=ms[:, b : b + 1])
             nc.scalar.activation(out=ms[:, 2:3], in_=ms[:, 1:2], func=ACT.Identity, bias=EPS, scale=1.0)
-            nc.scalar.activation(out=ms[:, 3:4], in_=ms[:, 0:1], func=ACT.Sqrt, bias=ms[:, 2:3], scale=1.0)
-            rstd = small.tile([P, 1], F32, name="rstd", tag="rstd")
-            nc.vector.reciprocal(out=rstd[:], in_=ms[:, 3:4])
+            nc.scalar.activation(out=ms[:, 3:4], in_=ms[:, 0:1], func=ACT.Abs_reciprocal_sqrt, bias=ms[:, 2:3], scale=1.0)
+            live[u] = (tps, ms)
 
+        def back(u):
+            s = u // 4
+            r = u % 4
+            c = s // 2
+            qk = s % 2
+            tps, ms = live[u]
+            rstd = ms[:, 3:4]
             m1 = work.tile([P, D], F32, name="m1", tag="m1")
             m2 = work.tile([P, D], F32, name="m2", tag="m2")
             ms12 = (m1, m2)
@@ -240,11 +254,11 @@ def tile_causalwanselfattention_pa_kernel(tc, x, wq, bq, wk, bk, gq, gk, freqs, 
                 for which in range(2):
                     mv = ms12[which][:].rearrange("p (h d) -> p h d", h=8)[:, 4 * b : 4 * b + 4, :]
                     nc.vector.scalar_tensor_tensor(
-                        out=mv[:, :, 0:FC], in0=tpv[:, :, 0:FC], scalar=rstd[:, 0:1], in1=tf[c][:, which, h0 : h0 + 4, :],
+                        out=mv[:, :, 0:FC], in0=tpv[:, :, 0:FC], scalar=rstd, in1=tf[c][:, which, h0 : h0 + 4, :],
                         op0=ALU.mult, op1=ALU.mult,
                     )
                     nc.vector.scalar_tensor_tensor(
-                        out=mv[:, :, FC:P], in0=tpv[:, :, FC:P], scalar=rstd[:, 0:1], in1=thw[r][:, which, h0 : h0 + 4, :],
+                        out=mv[:, :, FC:P], in0=tpv[:, :, FC:P], scalar=rstd, in1=thw[r][:, which, h0 : h0 + 4, :],
                         op0=ALU.mult, op1=ALU.mult,
                     )
             o = outp.tile([P, D], F32, name="o", tag="o")
@@ -257,26 +271,29 @@ def tile_causalwanselfattention_pa_kernel(tc, x, wq, bq, wk, bk, gq, gk, freqs, 
             i = 4 * c + r
             nc.sync.dma_start(out=outs[qk][P * i : P * (i + 1), :], in_=o[:])
 
-        for s in range(9):
-            for r in range(4):
-                if s < 8:
-                    mxe(s, 2 * r)
-                    mxe(s, 2 * r + 1)
-                if s == 0:
-                    if r % 2 == 0:
-                        new_group(("w", 2 + r // 2))
-                    for ft in (8 + 2 * r, 9 + 2 * r):
-                        turn_w(ft)
-                        load_x(ft)
-                    if r % 2 == 1:
-                        quantize(("w", 2 + r // 2), wc, ws, "w")
-                if s in (1, 3, 5):
-                    c = (s + 1) // 2
-                    if r == 0:
-                        new_group(("x", c))
-                    turn_x(c, r)
-                    if r == 3:
-                        quantize(("x", c), xc, xs, "x")
-                    table_g(tf[c], c, 0, FC, r % 2, 8 * (r // 2))
-                if s >= 1:
-                    unit(s - 1, r)
+        for n in range(32 + LAG_BACK):
+            if n < 32:
+                mxe(n // 4, 2 * (n % 4))
+                mxe(n // 4, 2 * (n % 4) + 1)
+            if n < 4:
+                if n % 2 == 0:
+                    new_group(("w", 2 + n // 2))
+                for ft in (8 + 2 * n, 9 + 2 * n):
+                    turn_w(ft, 2 + ft % 2, False)
+                    load_x(ft)
+                if n % 2 == 1:
+                    quantize(("w", 2 + n // 2), wc, ws, "w")
+            c = (n + 6) // 8
+            k = (n + 6) % 8
+            if 1 <= c <= 3:
+                if k == 0:
+                    new_group(("x", c))
+                if k < 4:
+                    turn_x(c, k, next_mm_bank(), False)
+                    table_g(tf[c], c, 0, FC, k % 2, 8 * (k // 2))
+                if k == 4:
+                    quantize(("x", c), xc, xs, "x")
+            if 0 <= n - LAG_FRONT < 32:
+                front(n - LAG_FRONT)
+            if 0 <= n - LAG_BACK < 32:
+                back(n - LAG_BACK)

@@ -35,7 +35,7 @@ def tile_causalwanselfattention_pa_kernel(tc, x, wq, bq, wk, bk, gq, gk, freqs, 
         keep = ctx.enter_context(tc.tile_pool(name="keep", bufs=1))
         ttp = ctx.enter_context(tc.tile_pool(name="ttp", bufs=16))
         work = ctx.enter_context(tc.tile_pool(name="work", bufs=3))
-        outp = ctx.enter_context(tc.tile_pool(name="outp", bufs=3))
+        outp = ctx.enter_context(tc.tile_pool(name="outp", bufs=5))
         small = ctx.enter_context(tc.tile_pool(name="small", bufs=4))
         psum = ctx.enter_context(tc.psum_pool(name="psum", bufs=1))
 
@@ -175,7 +175,7 @@ def tile_causalwanselfattention_pa_kernel(tc, x, wq, bq, wk, bk, gq, gk, freqs, 
         for grp in range(2):
             new_group(("w", grp))
             for a in range(4):
-                turn_w(4 * grp + a, a, a % 2 == 0)
+                turn_w(4 * grp + a, a, False)
                 if grp == 0:
                     load_w(12 + a)
                 else:
@@ -187,20 +187,22 @@ def tile_causalwanselfattention_pa_kernel(tc, x, wq, bq, wk, bk, gq, gk, freqs, 
         for r in range(4):
             for b in range(2):
                 table_v(thw[r], r, FC, P, b)
-        for which in range(2):
-            table_g(tf[0], 0, 0, FC, which, 8)
-        for r in range(4):
+        for b in range(2, 4):
+            table_v(tf[0], 0, 0, FC, b)
+            table_v(thw[0], 0, FC, P, b)
+        for r in range(1, 4):
             for which in range(2):
                 table_g(thw[r], r, FC, P, which, 8)
 
         tts = {}
+        accs = {}
         mmb = {"n": 0}
 
         def next_mm_bank():
             mmb["n"] += 1
             return mmb["n"] % 2
 
-        def mxe(s, h):
+        def mx_pe(s, h):
             c = s // 2
             ft = 8 * (s % 2) + h
             col = (2 * (ft % 4)) * P
@@ -215,13 +217,17 @@ def tile_causalwanselfattention_pa_kernel(tc, x, wq, bq, wk, bk, gq, gk, freqs, 
                     start=(g == 0),
                     stop=(g == 1),
                 )
+            accs[(s, h)] = acc
+
+        def mx_evac(s, h):
+            ft = 8 * (s % 2) + h
             tt = ttp.tile([P, 512], F32, name="tt", tag="tt")
-            nc.scalar.activation(out=tt[:], in_=acc[:], func=ACT.Identity, bias=bcol[:, ft : ft + 1], scale=1.0)
+            nc.scalar.activation(out=tt[:], in_=accs[(s, h)][:], func=ACT.Identity, bias=bcol[:, ft : ft + 1], scale=1.0)
             tts[(s, h)] = tt
 
         live = {}
 
-        def front(u):
+        def front_pe(u):
             s = u // 4
             r = u % 4
             tps = []
@@ -231,12 +237,21 @@ def tile_causalwanselfattention_pa_kernel(tc, x, wq, bq, wk, bk, gq, gk, freqs, 
                     nc.tensor.transpose(tp[:, P * hh : P * (hh + 1)], tts[(s, 4 * b + hh)][:, P * r : P * (r + 1)], identf[:])
                 tps.append(tp)
             ms = small.tile([P, 4], F32, name="ms", tag="ms")
+            live[u] = (tps, ms)
+
+        def squares(u):
+            tps, ms = live[u]
             for b in range(2):
                 junk = work.tile([P, 512], BF16, name="junk", tag="junk")
                 nc.scalar.activation(out=junk[:], in_=tps[b][:], func=ACT.Square, scale=1.0 / 32.0, accum_out=ms[:, b : b + 1])
+
+        def tiny_a(u):
+            ms = live[u][1]
             nc.scalar.activation(out=ms[:, 2:3], in_=ms[:, 1:2], func=ACT.Identity, bias=EPS, scale=1.0)
+
+        def tiny_b(u):
+            ms = live[u][1]
             nc.scalar.activation(out=ms[:, 3:4], in_=ms[:, 0:1], func=ACT.Abs_reciprocal_sqrt, bias=ms[:, 2:3], scale=1.0)
-            live[u] = (tps, ms)
 
         def back(u):
             s = u // 4
@@ -245,7 +260,7 @@ def tile_causalwanselfattention_pa_kernel(tc, x, wq, bq, wk, bk, gq, gk, freqs, 
             qk = s % 2
             tps, ms = live[u]
             rstd = ms[:, 3:4]
-            m1 = work.tile([P, D], F32, name="m1", tag="m1")
+            m1 = outp.tile([P, D], F32, name="m1", tag="m1")
             m2 = work.tile([P, D], F32, name="m2", tag="m2")
             ms12 = (m1, m2)
             for b in range(2):
@@ -261,39 +276,51 @@ def tile_causalwanselfattention_pa_kernel(tc, x, wq, bq, wk, bk, gq, gk, freqs, 
                         out=mv[:, :, FC:P], in0=tpv[:, :, FC:P], scalar=rstd, in1=thw[r][:, which, h0 : h0 + 4, :],
                         op0=ALU.mult, op1=ALU.mult,
                     )
-            o = outp.tile([P, D], F32, name="o", tag="o")
-            nc.gpsimd.tensor_tensor(
-                out=o[:].rearrange("p (c t) -> p c t", t=2),
+            adder = nc.vector if u == 31 else nc.gpsimd
+            adder.tensor_tensor(
+                out=m1[:].rearrange("p (c t) -> p c t", t=2),
                 in0=m1[:].rearrange("p (c t) -> p c t", t=2),
                 in1=m2[:].rearrange("p (c t) -> p c t", t=2)[:, :, ::-1],
                 op=ALU.add,
             )
             i = 4 * c + r
-            nc.sync.dma_start(out=outs[qk][P * i : P * (i + 1), :], in_=o[:])
+            nc.sync.dma_start(out=outs[qk][P * i : P * (i + 1), :], in_=m1[:])
 
-        for n in range(32 + LAG_BACK):
-            if n < 32:
-                mxe(n // 4, 2 * (n % 4))
-                mxe(n // 4, 2 * (n % 4) + 1)
-            if n < 4:
-                if n % 2 == 0:
-                    new_group(("w", 2 + n // 2))
-                for ft in (8 + 2 * n, 9 + 2 * n):
-                    turn_w(ft, 2 + ft % 2, False)
-                    load_x(ft)
-                if n % 2 == 1:
-                    quantize(("w", 2 + n // 2), wc, ws, "w")
-            c = (n + 6) // 8
-            k = (n + 6) % 8
-            if 1 <= c <= 3:
-                if k == 0:
-                    new_group(("x", c))
-                if k < 4:
-                    turn_x(c, k, next_mm_bank(), False)
-                    table_g(tf[c], c, 0, FC, k % 2, 8 * (k // 2))
-                if k == 4:
-                    quantize(("x", c), xc, xs, "x")
-            if 0 <= n - LAG_FRONT < 32:
-                front(n - LAG_FRONT)
-            if 0 <= n - LAG_BACK < 32:
-                back(n - LAG_BACK)
+        with tc.manual_schedule(engines={mybir.EngineType.Activation}):
+            for n in range(32 + LAG_BACK):
+                u = n - LAG_FRONT
+                if n < 32:
+                    mx_pe(n // 4, 2 * (n % 4))
+                    mx_pe(n // 4, 2 * (n % 4) + 1)
+                if 0 <= u < 32:
+                    front_pe(u)
+                if n < 32:
+                    mx_evac(n // 4, 2 * (n % 4))
+                if 0 <= u - 1 < 32:
+                    tiny_a(u - 1)
+                if n < 32:
+                    mx_evac(n // 4, 2 * (n % 4) + 1)
+                if 0 <= u - 1 < 32:
+                    tiny_b(u - 1)
+                if 0 <= u < 32:
+                    squares(u)
+                if n < 4:
+                    if n % 2 == 0:
+                        new_group(("w", 2 + n // 2))
+                    for ft in (8 + 2 * n, 9 + 2 * n):
+                        turn_w(ft, 2 + ft % 2, False)
+                        load_x(ft)
+                    if n % 2 == 1:
+                        quantize(("w", 2 + n // 2), wc, ws, "w")
+                c = (n + 6) // 8
+                k = (n + 6) % 8
+                if 1 <= c <= 3:
+                    if k == 0:
+                        new_group(("x", c))
+                    if k < 4:
+                        turn_x(c, k, next_mm_bank(), False)
+                        table_g(tf[c], c, 0, FC, k % 2, 8 * (k // 2))
+                    if k == 4:
+                        quantize(("x", c), xc, xs, "x")
+                if 0 <= n - LAG_BACK < 32:
+                    back(n - LAG_BACK)

@@ -227,23 +227,21 @@ def tile_causalwanselfattention_pa_kernel(tc, x, wq, bq, wk, bk, gq, gk, freqs, 
 
         live = {}
 
-        def front_pe(u):
+        def front_pe(u, b):
             s = u // 4
             r = u % 4
-            tps = []
-            for b in range(2):
-                tp = bank(2 + 2 * (u % 3) + b, [P, 512], F32)
-                for hh in range(4):
-                    nc.tensor.transpose(tp[:, P * hh : P * (hh + 1)], tts[(s, 4 * b + hh)][:, P * r : P * (r + 1)], identf[:])
-                tps.append(tp)
-            ms = small.tile([P, 4], F32, name="ms", tag="ms")
-            live[u] = (tps, ms)
+            if b == 0:
+                ms = small.tile([P, 4], F32, name="ms", tag="ms")
+                live[u] = ([], ms)
+            tp = bank(2 + 2 * (u % 3) + b, [P, 512], F32)
+            for hh in range(4):
+                nc.tensor.transpose(tp[:, P * hh : P * (hh + 1)], tts[(s, 4 * b + hh)][:, P * r : P * (r + 1)], identf[:])
+            live[u][0].append(tp)
 
-        def squares(u):
+        def square(u, b):
             tps, ms = live[u]
-            for b in range(2):
-                junk = work.tile([P, 512], BF16, name="junk", tag="junk")
-                nc.scalar.activation(out=junk[:], in_=tps[b][:], func=ACT.Square, scale=1.0 / 32.0, accum_out=ms[:, b : b + 1])
+            junk = work.tile([P, 512], BF16, name="junk", tag="junk")
+            nc.scalar.activation(out=junk[:], in_=tps[b][:], func=ACT.Square, scale=1.0 / 32.0, accum_out=ms[:, b : b + 1])
 
         def tiny_a(u):
             ms = live[u][1]
@@ -286,24 +284,29 @@ def tile_causalwanselfattention_pa_kernel(tc, x, wq, bq, wk, bk, gq, gk, freqs, 
             i = 4 * c + r
             nc.sync.dma_start(out=outs[qk][P * i : P * (i + 1), :], in_=m1[:])
 
-        with tc.manual_schedule(engines={mybir.EngineType.Activation}):
+        with tc.manual_schedule(engines={mybir.EngineType.Activation, mybir.EngineType.PE}):
             for n in range(32 + LAG_BACK):
                 u = n - LAG_FRONT
                 if n < 32:
                     mx_pe(n // 4, 2 * (n % 4))
+                if 0 <= u < 32:
+                    front_pe(u, 0)
+                if n < 32:
                     mx_pe(n // 4, 2 * (n % 4) + 1)
                 if 0 <= u < 32:
-                    front_pe(u)
+                    front_pe(u, 1)
                 if n < 32:
                     mx_evac(n // 4, 2 * (n % 4))
                 if 0 <= u - 1 < 32:
                     tiny_a(u - 1)
+                if 0 <= u < 32:
+                    square(u, 0)
                 if n < 32:
                     mx_evac(n // 4, 2 * (n % 4) + 1)
                 if 0 <= u - 1 < 32:
                     tiny_b(u - 1)
                 if 0 <= u < 32:
-                    squares(u)
+                    square(u, 1)
                 if n < 4:
                     if n % 2 == 0:
                         new_group(("w", 2 + n // 2))

@@ -245,11 +245,11 @@ def tile_causalwanselfattention_pa_kernel(tc, x, wq, bq, wk, bk, gq, gk, freqs, 
 
         def tiny_a(u):
             ms = live[u][1]
-            nc.scalar.activation(out=ms[:, 2:3], in_=ms[:, 1:2], func=ACT.Identity, bias=EPS, scale=1.0)
+            nc.scalar.activation(out=ms[:, 2:3], in_=ms[:, 0:1], func=ACT.Identity, bias=EPS, scale=1.0)
 
         def tiny_b(u):
             ms = live[u][1]
-            nc.scalar.activation(out=ms[:, 3:4], in_=ms[:, 0:1], func=ACT.Abs_reciprocal_sqrt, bias=ms[:, 2:3], scale=1.0)
+            nc.scalar.activation(out=ms[:, 3:4], in_=ms[:, 1:2], func=ACT.Abs_reciprocal_sqrt, bias=ms[:, 2:3], scale=1.0)
 
         def back(u):
             s = u // 4
@@ -298,13 +298,13 @@ def tile_causalwanselfattention_pa_kernel(tc, x, wq, bq, wk, bk, gq, gk, freqs, 
                 if n < 32:
                     mx_evac(n // 4, 2 * (n % 4))
                 if 0 <= u - 1 < 32:
-                    tiny_a(u - 1)
+                    tiny_b(u - 1)
                 if 0 <= u < 32:
                     square(u, 0)
                 if n < 32:
                     mx_evac(n // 4, 2 * (n % 4) + 1)
-                if 0 <= u - 1 < 32:
-                    tiny_b(u - 1)
+                if 0 <= u < 32:
+                    tiny_a(u)
                 if 0 <= u < 32:
                     square(u, 1)
                 if n < 4:

from contextlib import ExitStack

import concourse.mybir as mybir
from concourse.masks import make_identity

F32 = mybir.dt.float32
BF16 = mybir.dt.bfloat16
U32 = mybir.dt.uint32
U8 = mybir.dt.uint8
E5X4 = mybir.dt.float8_e5m2_x4
ALU = mybir.AluOpType
ACT = mybir.ActivationFunctionType

P = 128
L = 2048
D = 1024
EPS = 1.0e-6
FC = 44
HC = 86
FLOPS = 2 * L * D * 2 * D
LAG_FRONT = 4
LAG_BACK = 5


def tile_causalwanselfattention_pa_kernel(tc, x, wq, bq, wk, bk, gq, gk, freqs, out_0, out_1):
    nc = tc.nc
    xf = x.flatten_outer_dims()
    outs = (out_0.rearrange("b l h d -> (b l) (h d)"), out_1.rearrange("b l h d -> (b l) (h d)"))
    wsrc = (wq, wk)

    with ExitStack() as ctx:
        const = ctx.enter_context(tc.tile_pool(name="const", bufs=1))
        rawp = ctx.enter_context(tc.tile_pool(name="rawp", bufs=12))
        grpp = ctx.enter_context(tc.tile_pool(name="grpp", bufs=2))
        keep = ctx.enter_context(tc.tile_pool(name="keep", bufs=1))
        ttp = ctx.enter_context(tc.tile_pool(name="ttp", bufs=16))
        work = ctx.enter_context(tc.tile_pool(name="work", bufs=3))
        outp = ctx.enter_context(tc.tile_pool(name="outp", bufs=5))
        small = ctx.enter_context(tc.tile_pool(name="small", bufs=4))
        psum = ctx.enter_context(tc.psum_pool(name="psum", bufs=1))

        def bank(n, shape, dtype):
            return psum.tile(shape, dtype, name="bank%d" % n, tag="bank%d" % n)

        misc = const.tile([P, P], BF16, name="misc")
        for i, v in enumerate((bq, bk, gq, gk)):
            nc.scalar.dma_start(out=misc[8 * i : 8 * i + 8, :], in_=v.rearrange("(r c) -> r c", c=P))
        fr = const.tile([P, P], BF16, name="fr")
        nc.scalar.dma_start(out=fr[:], in_=freqs[0:P].rearrange("p j t -> p (j t)"))
        nc.vector.memset(misc[32:64, :], 0.0)
        nc.vector.memset(misc[64:128, :], 0.0)
        one = const.tile([P, 1], F32, name="one")
        nc.vector.memset(one[:], 1.0)
        warm = const.tile([P, 1], F32, name="warm")
        nc.scalar.activation(out=warm[:], in_=one[:], func=ACT.Abs_reciprocal_sqrt)

        identf = const.tile([P, P], F32, name="identf")
        make_identity(nc, identf[:])
        identb = const.tile([P, P], BF16, name="identb")
        make_identity(nc, identb[:])

        raws = {}

        def load(key, rows):
            t = rawp.tile([P, D], BF16, name="raw", tag="raw")
            nc.sync.dma_start(out=t[:], in_=rows)
            raws[key] = t

        def load_x(i):
            load(("x", i), xf[P * i : P * (i + 1), :])

        def load_w(ft):
            load(("w", ft), wsrc[ft // 8][P * (ft % 8) : P * (ft % 8 + 1), :])

        for i in range(4):
            load_x(i)
        for ft in range(8):
            load_w(ft)

        def turn(key, dst_words, n, on_vector):
            words = raws[key][:].bitcast(F32)
            ps = bank(n, [P, 2, 2, P], F32)
            for g in range(2):
                for u in range(2):
                    nc.tensor.transpose(ps[:, g, u, :], words[:, 256 * g + u : 256 * (g + 1) : 2], identf[:])
            src = ps[:].rearrange("p g u r -> p g r u")
            if on_vector:
                nc.vector.tensor_copy(out=dst_words, in_=src)
            else:
                nc.scalar.copy(out=dst_words, in_=src)

        grps = {}
        xc = {}
        xs = {}
        wc = {}
        ws = {}

        def new_group(key):
            grps[key] = grpp.tile([P, 4096], BF16, name="grp", tag="grp", align_bytes=64)

        def turn_x(c, r, n, on_vector):
            gw = grps[("x", c)][:].bitcast(F32).rearrange("p (g t u) -> p g t u", g=2, u=2)
            turn(("x", 4 * c + r), gw[:, :, P * r : P * (r + 1), :], n, on_vector)

        def turn_w(ft, n, on_vector):
            gw = grps[("w", ft // 4)][:].bitcast(F32).rearrange("p (a g m u) -> p a g m u", a=4, g=2, u=2)
            turn(("w", ft), gw[:, ft % 4], n, on_vector)

        def quantize(key, codes, scales, nm):
            codes[key[1]] = keep.tile([P, 1024], U32, name="c_%s%d" % (nm, key[1]), align_bytes=64)
            scales[key[1]] = keep.tile([P, 1024], U8, name="s_%s%d" % (nm, key[1]), align_bytes=64)
            nc.vector.quantize_mx(out=codes[key[1]][:].bitcast(E5X4), scales=scales[key[1]][:], in_=grps[key][:])

        new_group(("x", 0))
        for r in range(4):
            turn_x(0, r, r, r % 2 == 0)
            load_w(8 + r)
        quantize(("x", 0), xc, xs, "x")

        selw = const.tile([P, 4, 32], BF16, name="selw")
        nc.vector.tensor_copy(out=selw[:], in_=identb[:, 0:32].unsqueeze(1).to_broadcast([P, 4, 32]))
        selh = const.tile([P, 16, 32], BF16, name="selh")
        nc.vector.tensor_copy(out=selh[:], in_=identb[:, 0:16].unsqueeze(2).to_broadcast([P, 16, 32]))

        bt_ps = bank(4, [P, P], BF16)
        nc.tensor.transpose(bt_ps[:], misc[:], identb[:])
        bcol = const.tile([P, 16], F32, name="bcol")
        nc.vector.tensor_copy(out=bcol[:], in_=bt_ps[:, 0:16])

        cs_ps = bank(5, [P, 4, P], F32)
        for r in range(4):
            nc.tensor.matmul(cs_ps[:, r, 0:FC], lhsT=identb[:, r : r + 1].to_broadcast([P, P]), rhs=fr[:, 0:FC], start=True, stop=True)
            nc.tensor.matmul(cs_ps[:, r, FC:HC], lhsT=selh[:, 4 * r : 4 * r + 4, :].rearrange("k a w -> k (a w)"), rhs=fr[:, FC:HC], start=True, stop=True)
            nc.tensor.matmul(cs_ps[:, r, HC:P], lhsT=selw[:].rearrange("k a w -> k (a w)"), rhs=fr[:, HC:P], start=True, stop=True)
        cc = const.tile([P, 4, P], F32, name="cc")
        ss = const.tile([P, 4, P], F32, name="ss")
        csv = cs_ps[:].rearrange("p r (j t) -> p (r j) t", t=2)
        ssv = ss[:].rearrange("p r (j t) -> p (r j) t", t=2)
        nc.vector.tensor_copy(out=cc[:].rearrange("p r (j t) -> p (r j) t", t=2), in_=csv[:, :, 0:1].to_broadcast([P, 256, 2]))
        nc.vector.tensor_copy(out=ssv[:, :, 0:1], in_=csv[:, :, 1:2])
        nc.vector.tensor_scalar_mul(out=ssv[:, :, 1:2], in0=csv[:, :, 1:2], scalar1=-1.0)
        trig = (cc, ss)

        g_ps = {}
        gb = const.tile([P, 16, P], F32, name="gb")
        for b, n in ((0, 6), (1, 7), (2, 4), (3, 5)):
            gp = bank(n, [P, 4, P], F32)
            for hh in range(4):
                i = 16 + 4 * b + hh
                nc.tensor.matmul(gp[:, hh, :], lhsT=identb[:, i : i + 1].to_broadcast([P, P]), rhs=misc[:], start=True, stop=True)
            g_ps[b] = gp
        for b in (2, 3, 0, 1):
            nc.scalar.copy(out=gb[:, 4 * b : 4 * b + 4, :], in_=g_ps[b][:])

        tf = [const.tile([P, 2, 16, FC], F32, name="tf%d" % f) for f in range(4)]
        thw = [const.tile([P, 2, 16, P - FC], F32, name="thw%d" % r) for r in range(4)]

        def table_v(dst, v, lo, hi, b):
            for which in range(2):
                nc.vector.tensor_tensor(
                    out=dst[:, which, 4 * b : 4 * b + 4, :],
                    in0=g_ps[b][:, :, lo:hi],
                    in1=trig[which][:, v, lo:hi].unsqueeze(1).to_broadcast([P, 4, hi - lo]),
                    op=ALU.mult,
                )

        def table_g(dst, v, lo, hi, which, h0):
            nc.gpsimd.tensor_tensor(
                out=dst[:, which, h0 : h0 + 8, :],
                in0=gb[:, h0 : h0 + 8, lo:hi],
                in1=trig[which][:, v, lo:hi].unsqueeze(1).to_broadcast([P, 8, hi - lo]),
                op=ALU.mult,
            )

        for grp in range(2):
            new_group(("w", grp))
            for a in range(4):
                turn_w(4 * grp + a, a, False)
                if grp == 0:
                    load_w(12 + a)
                else:
                    load_x(4 + a)
            quantize(("w", grp), wc, ws, "w")

        for b in range(2):
            table_v(tf[0], 0, 0, FC, b)
        for r in range(4):
            for b in range(2):
                table_v(thw[r], r, FC, P, b)
        for b in range(2, 4):
            table_v(tf[0], 0, 0, FC, b)
            table_v(thw[0], 0, FC, P, b)
        for r in range(1, 4):
            for which in range(2):
                table_g(thw[r], r, FC, P, which, 8)

        tts = {}
        accs = {}
        mmb = {"n": 0}

        def next_mm_bank():
            mmb["n"] += 1
            return mmb["n"] % 2

        def mx_pe(s, h):
            c = s // 2
            ft = 8 * (s % 2) + h
            col = (2 * (ft % 4)) * P
            acc = bank(next_mm_bank(), [P, 512], F32)
            for g in range(2):
                nc.tensor.matmul_mx(
                    out=acc[:],
                    lhsT=wc[ft // 4][:, col + P * g : col + P * (g + 1)].bitcast(E5X4),
                    lhsT_scale=ws[ft // 4][:, col + P * g : col + P * (g + 1)],
                    rhs=xc[c][:, 512 * g : 512 * (g + 1)].bitcast(E5X4),
                    rhs_scale=xs[c][:, 512 * g : 512 * (g + 1)],
                    start=(g == 0),
                    stop=(g == 1),
                )
            accs[(s, h)] = acc

        def mx_evac(s, h):
            ft = 8 * (s % 2) + h
            tt = ttp.tile([P, 512], F32, name="tt", tag="tt")
            nc.scalar.activation(out=tt[:], in_=accs[(s, h)][:], func=ACT.Identity, bias=bcol[:, ft : ft + 1], scale=1.0)
            tts[(s, h)] = tt

        live = {}

        def front_pe(u, b):
            s = u // 4
            r = u % 4
            if b == 0:
                ms = small.tile([P, 4], F32, name="ms", tag="ms")
                live[u] = ([], ms)
            tp = bank(2 + 2 * (u % 3) + b, [P, 512], F32)
            for hh in range(4):
                nc.tensor.transpose(tp[:, P * hh : P * (hh + 1)], tts[(s, 4 * b + hh)][:, P * r : P * (r + 1)], identf[:])
            live[u][0].append(tp)

        def square(u, b):
            tps, ms = live[u]
            junk = work.tile([P, 512], BF16, name="junk", tag="junk")
            nc.scalar.activation(out=junk[:], in_=tps[b][:], func=ACT.Square, scale=1.0 / 32.0, accum_out=ms[:, b : b + 1])

        def tiny_a(u):
            ms = live[u][1]
            nc.scalar.activation(out=ms[:, 2:3], in_=ms[:, 0:1], func=ACT.Identity, bias=EPS, scale=1.0)

        def tiny_b(u):
            ms = live[u][1]
            nc.scalar.activation(out=ms[:, 3:4], in_=ms[:, 1:2], func=ACT.Abs_reciprocal_sqrt, bias=ms[:, 2:3], scale=1.0)

        def back(u):
            s = u // 4
            r = u % 4
            c = s // 2
            qk = s % 2
            tps, ms = live[u]
            rstd = ms[:, 3:4]
            m1 = outp.tile([P, D], F32, name="m1", tag="m1")
            m2 = work.tile([P, D], F32, name="m2", tag="m2")
            ms12 = (m1, m2)
            for b in range(2):
                tpv = tps[b][:].rearrange("p (h d) -> p h d", h=4)
                h0 = 8 * qk + 4 * b
                for which in range(2):
                    mv = ms12[which][:].rearrange("p (h d) -> p h d", h=8)[:, 4 * b : 4 * b + 4, :]
                    nc.vector.scalar_tensor_tensor(
                        out=mv[:, :, 0:FC], in0=tpv[:, :, 0:FC], scalar=rstd, in1=tf[c][:, which, h0 : h0 + 4, :],
                        op0=ALU.mult, op1=ALU.mult,
                    )
                    nc.vector.scalar_tensor_tensor(
                        out=mv[:, :, FC:P], in0=tpv[:, :, FC:P], scalar=rstd, in1=thw[r][:, which, h0 : h0 + 4, :],
                        op0=ALU.mult, op1=ALU.mult,
                    )
            adder = nc.vector if u == 31 else nc.gpsimd
            adder.tensor_tensor(
                out=m1[:].rearrange("p (c t) -> p c t", t=2),
                in0=m1[:].rearrange("p (c t) -> p c t", t=2),
                in1=m2[:].rearrange("p (c t) -> p c t", t=2)[:, :, ::-1],
                op=ALU.add,
            )
            i = 4 * c + r
            nc.sync.dma_start(out=outs[qk][P * i : P * (i + 1), :], in_=m1[:])

        with tc.manual_schedule(engines={mybir.EngineType.Activation, mybir.EngineType.PE}):
            for n in range(32 + LAG_BACK):
                u = n - LAG_FRONT
                if n < 32:
                    mx_pe(n // 4, 2 * (n % 4))
                if 0 <= u < 32:
                    front_pe(u, 0)
                if n < 32:
                    mx_pe(n // 4, 2 * (n % 4) + 1)
                if 0 <= u < 32:
                    front_pe(u, 1)
                if n < 32:
                    mx_evac(n // 4, 2 * (n % 4))
                if 0 <= u - 1 < 32:
                    tiny_b(u - 1)
                if 0 <= u < 32:
                    square(u, 0)
                if n < 32:
                    mx_evac(n // 4, 2 * (n % 4) + 1)
                if 0 <= u < 32:
                    tiny_a(u)
                if 0 <= u < 32:
                    square(u, 1)
                if n < 4:
                    if n % 2 == 0:
                        new_group(("w", 2 + n // 2))
                    for ft in (8 + 2 * n, 9 + 2 * n):
                        turn_w(ft, 2 + ft % 2, False)
                        load_x(ft)
                    if n % 2 == 1:
                        quantize(("w", 2 + n // 2), wc, ws, "w")
                c = (n + 6) // 8
                k = (n + 6) % 8
                if 1 <= c <= 3:
                    if k == 0:
                        new_group(("x", c))
                    if k < 4:
                        turn_x(c, k, next_mm_bank(), False)
                        table_g(tf[c], c, 0, FC, k % 2, 8 * (k // 2))
                    if k == 4:
                        quantize(("x", c), xc, xs, "x")
                if 0 <= n - LAG_BACK < 32:
                    back(n - LAG_BACK)
